import numpy as np
import ml_dtypes


def mxq(x, axis, fmt="e4m3"):
    dtype, down = {"e4m3": (ml_dtypes.float8_e4m3fn, 7), "e5m2": (ml_dtypes.float8_e5m2, 14)}[fmt]
    v = np.moveaxis(np.asarray(x, np.float32).astype(ml_dtypes.bfloat16).astype(np.float64), axis, -1)
    blocks = v.reshape(v.shape[:-1] + (-1, 32))
    amax = np.abs(blocks).max(-1, keepdims=True)
    byte = np.maximum(np.where(amax > 0, np.frexp(amax)[1] - 1 + 127, 0) - down, 1)
    scale = np.exp2(byte - 127.0)
    codes = (blocks / scale).astype(np.float32).astype(dtype).astype(np.float64)
    return np.moveaxis((codes * scale).reshape(v.shape), -1, axis)


WIDE = False


def mx_kscale(k):
    if not WIDE:
        return np.ones(k)
    levels = np.array([10, -10, 5, -5, 0])
    a = np.random.permutation(np.resize(levels, k // 512 * 4)).reshape(k // 512, 4)
    idx = np.arange(k)
    return np.exp2(a[idx // 512, idx % 128 // 32])


BF16 = ml_dtypes.bfloat16


def bf(x):
    return np.asarray(x, np.float32).astype(BF16)


def f64(x):
    return np.asarray(x).astype(np.float64)


E2M1 = np.array([0.0, 0.5, 1.0, 1.5, 2.0, 3.0, 4.0, 6.0, -0.0, -0.5, -1.0, -1.5, -2.0, -3.0, -4.0, -6.0])


def pack_weight(w, fmt):
    k, n = w.shape
    w = f64(bf(w)).reshape(k // 32, 32, n)
    amax = np.abs(w).max(1)
    if fmt == "e4m3":
        byte = np.frexp(amax)[1] - 1 + 127 - 7
    else:
        mant, ex = np.frexp(amax / 6.0)
        byte = np.where(mant > 0.5, ex, ex - 1) + 127
    byte = np.clip(np.where(amax > 0, byte, 1), 1, 254)
    scaled = (w * np.exp2(127.0 - byte)[:, None, :]).reshape(k, n).astype(np.float32)
    by_word = np.ascontiguousarray(scaled.reshape(k // 512, 128, 4, n).transpose(0, 1, 3, 2))
    if fmt == "e4m3":
        words = by_word.astype(ml_dtypes.float8_e4m3fn).view(np.uint8)
    else:
        c = by_word.astype(ml_dtypes.float4_e2m1fn).view(np.uint8) & 0xF
        words = c[..., 0::2] | (c[..., 1::2] << 4)
    return np.ascontiguousarray(words), np.ascontiguousarray(byte.astype(np.uint8).reshape(k // 512, 16, n))


def unpack_weight(words, scales, fmt):
    g, p, n, _ = words.shape
    if fmt == "e4m3":
        vals = np.ascontiguousarray(words).view(ml_dtypes.float8_e4m3fn).astype(np.float64)
    else:
        nib = np.empty((g, p, n, 4), np.uint8)
        nib[..., 0::2] = words & 0xF
        nib[..., 1::2] = words >> 4
        vals = E2M1[nib]
    vals = vals * np.repeat(np.exp2(scales.astype(np.float64) - 127.0), 8, axis=1)[..., None]
    return vals.transpose(0, 1, 3, 2).reshape(g * 512, n)


B, D, H = 256, 16384, 256


def sigmoid(v):
    return 1.0 / (1.0 + np.exp(-v))


def setup_inputs():
    s = mx_kscale(D)
    x = bf(np.random.standard_normal((B, D)) * s)
    w = np.random.standard_normal((4 * H, D)) * 1.5 / np.sqrt(D) / s[None, :]
    words, scales = pack_weight(np.ascontiguousarray(w.T), "e4m3")
    b_ih0 = bf(np.random.standard_normal(4 * H) * 0.3)
    b_hh0 = bf(np.random.standard_normal(4 * H) * 0.3)
    return {"x": x,
            "W_ih0_words": words,
            "W_ih0_scales": scales,
            "b_ih0": b_ih0,
            "b_hh0": b_hh0}


def reference(x, W_ih0_words, W_ih0_scales, b_ih0, b_hh0):
    wt = unpack_weight(W_ih0_words, W_ih0_scales, "e4m3")
    b = f64(b_ih0) + f64(b_hh0)
    xq = mxq(f64(x), 1, "e4m3")
    a_i = (xq @ wt[:, :H]) + b[:H]
    a_go = (xq @ wt[:, 2 * H:]) + b[2 * H:]
    a_g, a_o = a_go[:, :H], a_go[:, H:]
    c = sigmoid(a_i) * np.tanh(a_g)
    return sigmoid(a_o) * np.tanh(c)

@@ -1,0 +1,176 @@
+from contextlib import ExitStack
+
+import concourse.mybir as mybir
+from concourse.masks import make_identity
+
+F32 = mybir.dt.float32
+BF16 = mybir.dt.bfloat16
+I32 = mybir.dt.int32
+U32 = mybir.dt.uint32
+U8 = mybir.dt.uint8
+FP8X4 = mybir.dt.float8_e4m3fn_x4
+ACT = mybir.ActivationFunctionType
+
+P = 128
+PACK = 4
+K_PASS = P * PACK
+PAIRS = K_PASS // 2
+
+B, D, H = 256, 16384, 256
+ROW_TILES = B // P
+GROUPS = D // K_PASS
+CHUNK = 4
+CHUNKS = GROUPS // CHUNK
+PLANE_STEP = 4
+
+LOAD_BUFS = 6
+
+FLOPS = 2 * B * D * 3 * H
+BYTES = B * D * 2 + D * 3 * H + (D // 32) * 3 * H + 2 * 3 * H * 2 + B * H * 4
+
+
+def tile_lstmbaseline_pa_k_kernel(tc, x, W_ih0_words, W_ih0_scales, b_ih0, b_hh0, out):
+    nc = tc.nc
+
+    x_view = x.rearrange("(b p) k -> p b k", p=P)
+    w_view = W_ih0_words.rearrange("g p n t -> p g (n t)")
+
+    with ExitStack() as ctx:
+        consts = ctx.enter_context(tc.tile_pool(name="consts", bufs=1))
+        x_pool = ctx.enter_context(tc.tile_pool(name="x_pool", bufs=LOAD_BUFS))
+        w_pool = ctx.enter_context(tc.tile_pool(name="w_pool", bufs=LOAD_BUFS))
+        stage = ctx.enter_context(tc.tile_pool(name="stage", bufs=CHUNK))
+        codes = ctx.enter_context(tc.tile_pool(name="codes", bufs=3))
+        gates = ctx.enter_context(tc.tile_pool(name="gates", bufs=ROW_TILES))
+        sums = ctx.enter_context(tc.psum_pool(name="sums", bufs=1))
+        flips = ctx.enter_context(tc.psum_pool(name="flips", bufs=CHUNK))
+
+        def load_x(c):
+            x_rows = x_pool.tile([P, ROW_TILES, CHUNK * K_PASS], BF16)
+            nc.sync.dma_start(out=x_rows[:], in_=x_view[:, :, c * CHUNK * K_PASS : (c + 1) * CHUNK * K_PASS])
+            return x_rows
+
+        def load_w(c):
+            groups = slice(c * CHUNK, (c + 1) * CHUNK)
+            for quadrant in range(4):
+                nc.sync.dma_start(
+                    out=w_planes[32 * quadrant : 32 * quadrant + CHUNK * PLANE_STEP, c, :].bitcast(I32),
+                    in_=W_ih0_scales[groups, 4 * quadrant : 4 * quadrant + 4, :].bitcast(I32),
+                )
+            w_i = w_pool.tile([P, CHUNK, H], U32, align_bytes=64)
+            nc.sync.dma_start(out=w_i[:].bitcast(I32), in_=w_view[:, groups, 0 : PACK * H].bitcast(I32))
+            w_go = w_pool.tile([P, CHUNK, 2 * H], U32, align_bytes=64)
+            nc.sync.dma_start(out=w_go[:].bitcast(I32), in_=w_view[:, groups, PACK * 2 * H : PACK * 4 * H].bitcast(I32))
+            return w_i, w_go
+
+        def transpose_and_quantise(x_rows):
+            x_words = codes.tile([P, CHUNK, B], U32, align_bytes=64)
+            x_planes = codes.tile([P, CHUNK, B], U8, align_bytes=64)
+            banks = []
+            for j in range(CHUNK):
+                flipped = flips.tile([P, ROW_TILES, 2, P], F32)
+                for half in range(ROW_TILES):
+                    pairs = x_rows[:, half, :].bitcast(F32)
+                    for odd in range(2):
+                        nc.tensor.transpose(
+                            flipped[:, half, odd, :],
+                            pairs[:, j * PAIRS + odd : (j + 1) * PAIRS : 2],
+                            identity[:],
+                        )
+                banks.append(flipped)
+            for j in range(CHUNK):
+                grouped = stage.tile([P, ROW_TILES, P, PACK], BF16, align_bytes=64)
+                nc.scalar.copy(out=grouped[:].bitcast(F32), in_=banks[j][:].rearrange("p b u r -> p b r u"))
+                nc.vector.quantize_mx(
+                    out=x_words[:, j, :].bitcast(FP8X4),
+                    scales=x_planes[:, j, :],
+                    in_=grouped[:].rearrange("p b r t -> p (b r t)"),
+                )
+            return x_words, x_planes
+
+        def multiply(c, x_words, x_planes, w_i, w_go):
+            for half in range(ROW_TILES):
+                rows = slice(half * P, (half + 1) * P)
+                for j in range(CHUNK):
+                    g = c * CHUNK + j
+                    plane = w_planes[j * PLANE_STEP : P, c, :]
+                    nc.tensor.matmul_mx(
+                        out=sum_go[half][:],
+                        lhsT=x_words[:, j, rows].bitcast(FP8X4),
+                        lhsT_scale=x_planes[:, j, rows],
+                        rhs=w_go[:, j, :].bitcast(FP8X4),
+                        rhs_scale=plane[:, 2 * H : 4 * H],
+                        start=(g == 0),
+                        stop=(g == GROUPS - 1),
+                    )
+                    nc.tensor.matmul_mx(
+                        out=sum_i[half][:],
+                        lhsT=x_words[:, j, rows].bitcast(FP8X4),
+                        lhsT_scale=x_planes[:, j, rows],
+                        rhs=w_i[:, j, :].bitcast(FP8X4),
+                        rhs_scale=plane[:, 0:H],
+                        start=(g == 0),
+                        stop=(g == GROUPS - 1),
+                    )
+
+        sum_go = [sums.tile([P, 2 * H], F32, name="sum_go%d" % half) for half in range(ROW_TILES)]
+        sum_i = [sums.tile([P, H], F32, name="sum_i%d" % half) for half in range(ROW_TILES)]
+
+        with tc.manual_schedule():
+            x_tiles = {0: load_x(0), 1: load_x(1)}
+
+            bias_rows = consts.tile([P, 4 * H], BF16)
+            nc.vector.memset(bias_rows[:], 0.0)
+            nc.scalar.dma_start(out=bias_rows[0:1, :], in_=b_ih0.unsqueeze(0))
+            nc.scalar.dma_start(out=bias_rows[1:2, :], in_=b_hh0.unsqueeze(0))
+            ones = consts.tile([P, P], BF16)
+            nc.vector.memset(ones[:], 1.0)
+            bias_go_psum = flips.tile([P, 2 * H], F32, tag="flipped")
+            nc.tensor.matmul(out=bias_go_psum[:], lhsT=ones[:], rhs=bias_rows[:, 2 * H : 4 * H], start=True, stop=True)
+            bias_i_psum = flips.tile([P, H], F32, tag="flipped")
+            nc.tensor.matmul(out=bias_i_psum[:], lhsT=ones[:], rhs=bias_rows[:, 0:H], start=True, stop=True)
+
+            w_planes = consts.tile([P, CHUNKS, 4 * H], U8, align_bytes=64)
+            nc.vector.memset(w_planes[:].bitcast(I32), 0)
+            w_tiles = {0: load_w(0)}
+
+            identity = consts.tile([P, P], F32)
+            make_identity(nc, identity[:])
+
+            warm = consts.tile([P, 1], F32)
+            nc.vector.memset(warm[:], 0.0)
+            warmed = consts.tile([P, 1], F32)
+            nc.scalar.activation(out=warmed[:], in_=warm[:], func=ACT.Sigmoid)
+
+            bias_go = consts.tile([P, 2 * H], F32)
+            nc.vector.tensor_copy(out=bias_go[:], in_=bias_go_psum[:])
+            bias_i = consts.tile([P, H], F32)
+            nc.vector.tensor_copy(out=bias_i[:], in_=bias_i_psum[:])
+
+            x_codes = {0: transpose_and_quantise(x_tiles[0])}
+            for c in range(CHUNKS):
+                if c + 2 < CHUNKS:
+                    x_tiles[c + 2] = load_x(c + 2)
+                if c + 1 < CHUNKS:
+                    w_tiles[c + 1] = load_w(c + 1)
+                    x_codes[c + 1] = transpose_and_quantise(x_tiles[c + 1])
+                multiply(c, x_codes[c][0], x_codes[c][1], w_tiles[c][0], w_tiles[c][1])
+
+        for half in range(ROW_TILES):
+            a_i = gates.tile([P, H], F32)
+            nc.vector.tensor_add(out=a_i[:], in0=sum_i[half][:], in1=bias_i[:])
+            a_go = gates.tile([P, 2 * H], F32)
+            nc.vector.tensor_add(out=a_go[:], in0=sum_go[half][:], in1=bias_go[:])
+            gate_i = gates.tile([P, H], F32)
+            nc.scalar.activation(out=gate_i[:], in_=a_i[:], func=ACT.Sigmoid)
+            gate_g = gates.tile([P, H], F32)
+            nc.scalar.activation(out=gate_g[:], in_=a_go[:, 0:H], func=ACT.Tanh)
+            gate_o = gates.tile([P, H], F32)
+            nc.scalar.activation(out=gate_o[:], in_=a_go[:, H : 2 * H], func=ACT.Sigmoid)
+            cell = gates.tile([P, H], F32)
+            nc.vector.tensor_mul(out=cell[:], in0=gate_i[:], in1=gate_g[:])
+            tanh_cell = gates.tile([P, H], F32)
+            nc.scalar.activation(out=tanh_cell[:], in_=cell[:], func=ACT.Tanh)
+            hidden = gates.tile([P, H], F32)
+            nc.vector.tensor_mul(out=hidden[:], in0=gate_o[:], in1=tanh_cell[:])
+            nc.sync.dma_start(out=out[half * P : (half + 1) * P, :], in_=hidden[:])

@@ -57,10 +57,10 @@ def tile_lstmbaseline_pa_k_kernel(tc, x, W_ih0_words, W_ih0_scales, b_ih0, b_hh0
                     out=w_planes[32 * quadrant : 32 * quadrant + CHUNK * PLANE_STEP, c, :].bitcast(I32),
                     in_=W_ih0_scales[groups, 4 * quadrant : 4 * quadrant + 4, :].bitcast(I32),
                 )
-            w_i = w_pool.tile([P, CHUNK, H], U32, align_bytes=64)
-            nc.sync.dma_start(out=w_i[:].bitcast(I32), in_=w_view[:, groups, 0 : PACK * H].bitcast(I32))
             w_go = w_pool.tile([P, CHUNK, 2 * H], U32, align_bytes=64)
             nc.sync.dma_start(out=w_go[:].bitcast(I32), in_=w_view[:, groups, PACK * 2 * H : PACK * 4 * H].bitcast(I32))
+            w_i = w_pool.tile([P, CHUNK, H], U32, align_bytes=64)
+            nc.sync.dma_start(out=w_i[:].bitcast(I32), in_=w_view[:, groups, 0 : PACK * H].bitcast(I32))
             return w_i, w_go
 
         def transpose_and_quantise(x_rows):
@@ -93,22 +93,25 @@ def tile_lstmbaseline_pa_k_kernel(tc, x, W_ih0_words, W_ih0_scales, b_ih0, b_hh0
                 rows = slice(half * P, (half + 1) * P)
                 for j in range(CHUNK):
                     g = c * CHUNK + j
-                    plane = w_planes[j * PLANE_STEP : P, c, :]
                     nc.tensor.matmul_mx(
                         out=sum_go[half][:],
                         lhsT=x_words[:, j, rows].bitcast(FP8X4),
                         lhsT_scale=x_planes[:, j, rows],
                         rhs=w_go[:, j, :].bitcast(FP8X4),
-                        rhs_scale=plane[:, 2 * H : 4 * H],
+                        rhs_scale=w_planes[j * PLANE_STEP : P, c, 2 * H : 4 * H],
                         start=(g == 0),
                         stop=(g == GROUPS - 1),
                     )
+            for half in range(ROW_TILES):
+                rows = slice(half * P, (half + 1) * P)
+                for j in range(CHUNK):
+                    g = c * CHUNK + j
                     nc.tensor.matmul_mx(
                         out=sum_i[half][:],
                         lhsT=x_words[:, j, rows].bitcast(FP8X4),
                         lhsT_scale=x_planes[:, j, rows],
                         rhs=w_i[:, j, :].bitcast(FP8X4),
-                        rhs_scale=plane[:, 0:H],
+                        rhs_scale=w_planes[j * PLANE_STEP : P, c, 0:H],
                         start=(g == 0),
                         stop=(g == GROUPS - 1),
                     )
@@ -156,21 +159,25 @@ def tile_lstmbaseline_pa_k_kernel(tc, x, W_ih0_words, W_ih0_scales, b_ih0, b_hh0
                     x_codes[c + 1] = transpose_and_quantise(x_tiles[c + 1])
                 multiply(c, x_codes[c][0], x_codes[c][1], w_tiles[c][0], w_tiles[c][1])
 
-        for half in range(ROW_TILES):
-            a_i = gates.tile([P, H], F32)
-            nc.vector.tensor_add(out=a_i[:], in0=sum_i[half][:], in1=bias_i[:])
-            a_go = gates.tile([P, 2 * H], F32)
-            nc.vector.tensor_add(out=a_go[:], in0=sum_go[half][:], in1=bias_go[:])
-            gate_i = gates.tile([P, H], F32)
-            nc.scalar.activation(out=gate_i[:], in_=a_i[:], func=ACT.Sigmoid)
-            gate_g = gates.tile([P, H], F32)
-            nc.scalar.activation(out=gate_g[:], in_=a_go[:, 0:H], func=ACT.Tanh)
-            gate_o = gates.tile([P, H], F32)
-            nc.scalar.activation(out=gate_o[:], in_=a_go[:, H : 2 * H], func=ACT.Sigmoid)
-            cell = gates.tile([P, H], F32)
-            nc.vector.tensor_mul(out=cell[:], in0=gate_i[:], in1=gate_g[:])
-            tanh_cell = gates.tile([P, H], F32)
-            nc.scalar.activation(out=tanh_cell[:], in_=cell[:], func=ACT.Tanh)
-            hidden = gates.tile([P, H], F32)
-            nc.vector.tensor_mul(out=hidden[:], in0=gate_o[:], in1=tanh_cell[:])
-            nc.sync.dma_start(out=out[half * P : (half + 1) * P, :], in_=hidden[:])
+            a_go, gate_g, gate_o, a_i, gate_i, cell, tanh_cell, hidden = {}, {}, {}, {}, {}, {}, {}, {}
+            for half in range(ROW_TILES):
+                a_go[half] = gates.tile([P, 2 * H], F32, name="a_go")
+                nc.vector.tensor_add(out=a_go[half][:], in0=sum_go[half][:], in1=bias_go[:])
+                gate_g[half] = gates.tile([P, H], F32, name="gate_g")
+                nc.scalar.activation(out=gate_g[half][:], in_=a_go[half][:, 0:H], func=ACT.Tanh)
+                gate_o[half] = gates.tile([P, H], F32, name="gate_o")
+                nc.scalar.activation(out=gate_o[half][:], in_=a_go[half][:, H : 2 * H], func=ACT.Sigmoid)
+            for half in range(ROW_TILES):
+                a_i[half] = gates.tile([P, H], F32, name="a_i")
+                nc.vector.tensor_add(out=a_i[half][:], in0=sum_i[half][:], in1=bias_i[:])
+                gate_i[half] = gates.tile([P, H], F32, name="gate_i")
+                nc.scalar.activation(out=gate_i[half][:], in_=a_i[half][:], func=ACT.Sigmoid)
+            for half in range(ROW_TILES):
+                cell[half] = gates.tile([P, H], F32, name="cell")
+                nc.vector.tensor_mul(out=cell[half][:], in0=gate_i[half][:], in1=gate_g[half][:])
+                tanh_cell[half] = gates.tile([P, H], F32, name="tanh_cell")
+                nc.scalar.activation(out=tanh_cell[half][:], in_=cell[half][:], func=ACT.Tanh)
+            for half in range(ROW_TILES):
+                hidden[half] = gates.tile([P, H], F32, name="hidden")
+                nc.vector.tensor_mul(out=hidden[half][:], in0=gate_o[half][:], in1=tanh_cell[half][:])
+                nc.sync.dma_start(out=out[half * P : (half + 1) * P, :], in_=hidden[half][:])

@@ -53,9 +53,9 @@ def tile_lstmbaseline_pa_k_kernel(tc, x, W_ih0_words, W_ih0_scales, b_ih0, b_hh0
         def load_w(c):
             groups = slice(c * CHUNK, (c + 1) * CHUNK)
             for quadrant in range(4):
-                nc.sync.dma_start(
-                    out=w_planes[32 * quadrant : 32 * quadrant + CHUNK * PLANE_STEP, c, :].bitcast(I32),
-                    in_=W_ih0_scales[groups, 4 * quadrant : 4 * quadrant + 4, :].bitcast(I32),
+                nc.gpsimd.dma_start(
+                    out=w_planes[32 * quadrant : 32 * quadrant + CHUNK * PLANE_STEP, c, :].bitcast(F32),
+                    in_=W_ih0_scales[groups, 4 * quadrant : 4 * quadrant + 4, :].bitcast(F32),
                 )
             w_go = w_pool.tile([P, CHUNK, 2 * H], U32, align_bytes=64)
             nc.sync.dma_start(out=w_go[:].bitcast(I32), in_=w_view[:, groups, PACK * 2 * H : PACK * 4 * H].bitcast(I32))
@@ -135,10 +135,9 @@ def tile_lstmbaseline_pa_k_kernel(tc, x, W_ih0_words, W_ih0_scales, b_ih0, b_hh0
 
             w_planes = consts.tile([P, CHUNKS, 4 * H], U8, align_bytes=64)
             nc.vector.memset(w_planes[:].bitcast(I32), 0)
-            w_tiles = {0: load_w(0)}
-
             identity = consts.tile([P, P], F32)
             make_identity(nc, identity[:])
+            w_tiles = {0: load_w(0)}
 
             warm = consts.tile([P, 1], F32)
             nc.vector.memset(warm[:], 0.0)

@@ -14,7 +14,6 @@ ACT = mybir.ActivationFunctionType
 P = 128
 PACK = 4
 K_PASS = P * PACK
-PAIRS = K_PASS // 2
 
 B, D, H = 256, 16384, 256
 ROW_TILES = B // P
@@ -39,6 +38,7 @@ def tile_lstmbaseline_pa_k_kernel(tc, x, W_ih0_words, W_ih0_scales, b_ih0, b_hh0
         consts = ctx.enter_context(tc.tile_pool(name="consts", bufs=1))
         x_pool = ctx.enter_context(tc.tile_pool(name="x_pool", bufs=LOAD_BUFS))
         w_pool = ctx.enter_context(tc.tile_pool(name="w_pool", bufs=LOAD_BUFS))
+        sorted_pool = ctx.enter_context(tc.tile_pool(name="sorted_pool", bufs=3))
         stage = ctx.enter_context(tc.tile_pool(name="stage", bufs=CHUNK))
         codes = ctx.enter_context(tc.tile_pool(name="codes", bufs=3))
         gates = ctx.enter_context(tc.tile_pool(name="gates", bufs=ROW_TILES))
@@ -63,20 +63,23 @@ def tile_lstmbaseline_pa_k_kernel(tc, x, W_ih0_words, W_ih0_scales, b_ih0, b_hh0
             nc.sync.dma_start(out=w_i[:].bitcast(I32), in_=w_view[:, groups, 0 : PACK * H].bitcast(I32))
             return w_i, w_go
 
-        def transpose_and_quantise(x_rows):
+        def sort_pairs(x_rows):
+            x_sorted = sorted_pool.tile([P, ROW_TILES, CHUNK, 2, P], F32)
+            nc.vector.tensor_copy(
+                out=x_sorted[:],
+                in_=x_rows[:].bitcast(F32).rearrange("p b (j q u) -> p b j u q", j=CHUNK, u=2),
+            )
+            return x_sorted
+
+        def transpose_and_quantise(x_sorted):
             x_words = codes.tile([P, CHUNK, B], U32, align_bytes=64)
             x_planes = codes.tile([P, CHUNK, B], U8, align_bytes=64)
             banks = []
             for j in range(CHUNK):
                 flipped = flips.tile([P, ROW_TILES, 2, P], F32)
                 for half in range(ROW_TILES):
-                    pairs = x_rows[:, half, :].bitcast(F32)
                     for odd in range(2):
-                        nc.tensor.transpose(
-                            flipped[:, half, odd, :],
-                            pairs[:, j * PAIRS + odd : (j + 1) * PAIRS : 2],
-                            identity[:],
-                        )
+                        nc.tensor.transpose(flipped[:, half, odd, :], x_sorted[:, half, j, odd, :], identity[:])
                 banks.append(flipped)
             for j in range(CHUNK):
                 grouped = stage.tile([P, ROW_TILES, P, PACK], BF16, align_bytes=64)
@@ -120,7 +123,7 @@ def tile_lstmbaseline_pa_k_kernel(tc, x, W_ih0_words, W_ih0_scales, b_ih0, b_hh0
         sum_i = [sums.tile([P, H], F32, name="sum_i%d" % half) for half in range(ROW_TILES)]
 
         with tc.manual_schedule():
-            x_tiles = {0: load_x(0), 1: load_x(1)}
+            loaded_x = {0: load_x(0), 1: load_x(1), 2: load_x(2)}
 
             bias_rows = consts.tile([P, 4 * H], BF16)
             nc.vector.memset(bias_rows[:], 0.0)
@@ -137,7 +140,7 @@ def tile_lstmbaseline_pa_k_kernel(tc, x, W_ih0_words, W_ih0_scales, b_ih0, b_hh0
             nc.vector.memset(w_planes[:].bitcast(I32), 0)
             identity = consts.tile([P, P], F32)
             make_identity(nc, identity[:])
-            w_tiles = {0: load_w(0)}
+            loaded_w = {0: load_w(0)}
 
             warm = consts.tile([P, 1], F32)
             nc.vector.memset(warm[:], 0.0)
@@ -149,14 +152,17 @@ def tile_lstmbaseline_pa_k_kernel(tc, x, W_ih0_words, W_ih0_scales, b_ih0, b_hh0
             bias_i = consts.tile([P, H], F32)
             nc.vector.tensor_copy(out=bias_i[:], in_=bias_i_psum[:])
 
-            x_codes = {0: transpose_and_quantise(x_tiles[0])}
+            sorted_x = {0: sort_pairs(loaded_x[0]), 1: sort_pairs(loaded_x[1])}
+            coded_x = {0: transpose_and_quantise(sorted_x[0])}
             for c in range(CHUNKS):
-                if c + 2 < CHUNKS:
-                    x_tiles[c + 2] = load_x(c + 2)
+                if c + 3 < CHUNKS:
+                    loaded_x[c + 3] = load_x(c + 3)
                 if c + 1 < CHUNKS:
-                    w_tiles[c + 1] = load_w(c + 1)
-                    x_codes[c + 1] = transpose_and_quantise(x_tiles[c + 1])
-                multiply(c, x_codes[c][0], x_codes[c][1], w_tiles[c][0], w_tiles[c][1])
+                    loaded_w[c + 1] = load_w(c + 1)
+                    coded_x[c + 1] = transpose_and_quantise(sorted_x[c + 1])
+                if c + 2 < CHUNKS:
+                    sorted_x[c + 2] = sort_pairs(loaded_x[c + 2])
+                multiply(c, coded_x[c][0], coded_x[c][1], loaded_w[c][0], loaded_w[c][1])
 
             a_go, gate_g, gate_o, a_i, gate_i, cell, tanh_cell, hidden = {}, {}, {}, {}, {}, {}, {}, {}
             for half in range(ROW_TILES):

@@ -14,6 +14,7 @@ ACT = mybir.ActivationFunctionType
 P = 128
 PACK = 4
 K_PASS = P * PACK
+PAIRS = K_PASS // 2
 
 B, D, H = 256, 16384, 256
 ROW_TILES = B // P
@@ -21,6 +22,7 @@ GROUPS = D // K_PASS
 CHUNK = 4
 CHUNKS = GROUPS // CHUNK
 PLANE_STEP = 4
+LOAD_GROUPS = 2
 
 LOAD_BUFS = 6
 
@@ -38,7 +40,6 @@ def tile_lstmbaseline_pa_k_kernel(tc, x, W_ih0_words, W_ih0_scales, b_ih0, b_hh0
         consts = ctx.enter_context(tc.tile_pool(name="consts", bufs=1))
         x_pool = ctx.enter_context(tc.tile_pool(name="x_pool", bufs=LOAD_BUFS))
         w_pool = ctx.enter_context(tc.tile_pool(name="w_pool", bufs=LOAD_BUFS))
-        sorted_pool = ctx.enter_context(tc.tile_pool(name="sorted_pool", bufs=3))
         stage = ctx.enter_context(tc.tile_pool(name="stage", bufs=CHUNK))
         codes = ctx.enter_context(tc.tile_pool(name="codes", bufs=3))
         gates = ctx.enter_context(tc.tile_pool(name="gates", bufs=ROW_TILES))
@@ -58,28 +59,35 @@ def tile_lstmbaseline_pa_k_kernel(tc, x, W_ih0_words, W_ih0_scales, b_ih0, b_hh0
                     in_=W_ih0_scales[groups, 4 * quadrant : 4 * quadrant + 4, :].bitcast(F32),
                 )
             w_go = w_pool.tile([P, CHUNK, 2 * H], U32, align_bytes=64)
-            nc.sync.dma_start(out=w_go[:].bitcast(I32), in_=w_view[:, groups, PACK * 2 * H : PACK * 4 * H].bitcast(I32))
+            for first in range(0, CHUNK, LOAD_GROUPS):
+                nc.sync.dma_start(
+                    out=w_go[:, first : first + LOAD_GROUPS, :].bitcast(I32),
+                    in_=w_view[
+                        :, c * CHUNK + first : c * CHUNK + first + LOAD_GROUPS, PACK * 2 * H : PACK * 4 * H
+                    ].bitcast(I32),
+                )
             w_i = w_pool.tile([P, CHUNK, H], U32, align_bytes=64)
-            nc.sync.dma_start(out=w_i[:].bitcast(I32), in_=w_view[:, groups, 0 : PACK * H].bitcast(I32))
+            for first in range(0, CHUNK, LOAD_GROUPS):
+                nc.sync.dma_start(
+                    out=w_i[:, first : first + LOAD_GROUPS, :].bitcast(I32),
+                    in_=w_view[:, c * CHUNK + first : c * CHUNK + first + LOAD_GROUPS, 0 : PACK * H].bitcast(I32),
+                )
             return w_i, w_go
 
-        def sort_pairs(x_rows):
-            x_sorted = sorted_pool.tile([P, ROW_TILES, CHUNK, 2, P], F32)
-            nc.vector.tensor_copy(
-                out=x_sorted[:],
-                in_=x_rows[:].bitcast(F32).rearrange("p b (j q u) -> p b j u q", j=CHUNK, u=2),
-            )
-            return x_sorted
-
-        def transpose_and_quantise(x_sorted):
+        def transpose_and_quantise(x_rows):
             x_words = codes.tile([P, CHUNK, B], U32, align_bytes=64)
             x_planes = codes.tile([P, CHUNK, B], U8, align_bytes=64)
             banks = []
             for j in range(CHUNK):
                 flipped = flips.tile([P, ROW_TILES, 2, P], F32)
                 for half in range(ROW_TILES):
+                    pairs = x_rows[:, half, :].bitcast(F32)
                     for odd in range(2):
-                        nc.tensor.transpose(flipped[:, half, odd, :], x_sorted[:, half, j, odd, :], identity[:])
+                        nc.tensor.transpose(
+                            flipped[:, half, odd, :],
+                            pairs[:, j * PAIRS + odd : (j + 1) * PAIRS : 2],
+                            identity[:],
+                        )
                 banks.append(flipped)
             for j in range(CHUNK):
                 grouped = stage.tile([P, ROW_TILES, P, PACK], BF16, align_bytes=64)
@@ -92,38 +100,40 @@ def tile_lstmbaseline_pa_k_kernel(tc, x, W_ih0_words, W_ih0_scales, b_ih0, b_hh0
             return x_words, x_planes
 
         def multiply(c, x_words, x_planes, w_i, w_go):
-            for half in range(ROW_TILES):
-                rows = slice(half * P, (half + 1) * P)
-                for j in range(CHUNK):
-                    g = c * CHUNK + j
-                    nc.tensor.matmul_mx(
-                        out=sum_go[half][:],
-                        lhsT=x_words[:, j, rows].bitcast(FP8X4),
-                        lhsT_scale=x_planes[:, j, rows],
-                        rhs=w_go[:, j, :].bitcast(FP8X4),
-                        rhs_scale=w_planes[j * PLANE_STEP : P, c, 2 * H : 4 * H],
-                        start=(g == 0),
-                        stop=(g == GROUPS - 1),
-                    )
-            for half in range(ROW_TILES):
-                rows = slice(half * P, (half + 1) * P)
-                for j in range(CHUNK):
-                    g = c * CHUNK + j
-                    nc.tensor.matmul_mx(
-                        out=sum_i[half][:],
-                        lhsT=x_words[:, j, rows].bitcast(FP8X4),
-                        lhsT_scale=x_planes[:, j, rows],
-                        rhs=w_i[:, j, :].bitcast(FP8X4),
-                        rhs_scale=w_planes[j * PLANE_STEP : P, c, 0:H],
-                        start=(g == 0),
-                        stop=(g == GROUPS - 1),
-                    )
+            for first in range(0, CHUNK, LOAD_GROUPS):
+                for half in range(ROW_TILES):
+                    rows = slice(half * P, (half + 1) * P)
+                    for j in range(first, first + LOAD_GROUPS):
+                        g = c * CHUNK + j
+                        nc.tensor.matmul_mx(
+                            out=sum_go[half][:],
+                            lhsT=x_words[:, j, rows].bitcast(FP8X4),
+                            lhsT_scale=x_planes[:, j, rows],
+                            rhs=w_go[:, j, :].bitcast(FP8X4),
+                            rhs_scale=w_planes[j * PLANE_STEP : P, c, 2 * H : 4 * H],
+                            start=(g == 0),
+                            stop=(g == GROUPS - 1),
+                        )
+            for first in range(0, CHUNK, LOAD_GROUPS):
+                for half in range(ROW_TILES):
+                    rows = slice(half * P, (half + 1) * P)
+                    for j in range(first, first + LOAD_GROUPS):
+                        g = c * CHUNK + j
+                        nc.tensor.matmul_mx(
+                            out=sum_i[half][:],
+                            lhsT=x_words[:, j, rows].bitcast(FP8X4),
+                            lhsT_scale=x_planes[:, j, rows],
+                            rhs=w_i[:, j, :].bitcast(FP8X4),
+                            rhs_scale=w_planes[j * PLANE_STEP : P, c, 0:H],
+                            start=(g == 0),
+                            stop=(g == GROUPS - 1),
+                        )
 
         sum_go = [sums.tile([P, 2 * H], F32, name="sum_go%d" % half) for half in range(ROW_TILES)]
         sum_i = [sums.tile([P, H], F32, name="sum_i%d" % half) for half in range(ROW_TILES)]
 
         with tc.manual_schedule():
-            loaded_x = {0: load_x(0), 1: load_x(1), 2: load_x(2)}
+            loaded_x = {0: load_x(0), 1: load_x(1)}
 
             bias_rows = consts.tile([P, 4 * H], BF16)
             nc.vector.memset(bias_rows[:], 0.0)
@@ -152,16 +162,13 @@ def tile_lstmbaseline_pa_k_kernel(tc, x, W_ih0_words, W_ih0_scales, b_ih0, b_hh0
             bias_i = consts.tile([P, H], F32)
             nc.vector.tensor_copy(out=bias_i[:], in_=bias_i_psum[:])
 
-            sorted_x = {0: sort_pairs(loaded_x[0]), 1: sort_pairs(loaded_x[1])}
-            coded_x = {0: transpose_and_quantise(sorted_x[0])}
+            coded_x = {0: transpose_and_quantise(loaded_x[0])}
             for c in range(CHUNKS):
-                if c + 3 < CHUNKS:
-                    loaded_x[c + 3] = load_x(c + 3)
+                if c + 2 < CHUNKS:
+                    loaded_x[c + 2] = load_x(c + 2)
                 if c + 1 < CHUNKS:
                     loaded_w[c + 1] = load_w(c + 1)
-                    coded_x[c + 1] = transpose_and_quantise(sorted_x[c + 1])
-                if c + 2 < CHUNKS:
-                    sorted_x[c + 2] = sort_pairs(loaded_x[c + 2])
+                    coded_x[c + 1] = transpose_and_quantise(loaded_x[c + 1])
                 multiply(c, coded_x[c][0], coded_x[c][1], loaded_w[c][0], loaded_w[c][1])
 
             a_go, gate_g, gate_o, a_i, gate_i, cell, tanh_cell, hidden = {}, {}, {}, {}, {}, {}, {}, {}

@@ -41,7 +41,7 @@ def tile_lstmbaseline_pa_k_kernel(tc, x, W_ih0_words, W_ih0_scales, b_ih0, b_hh0
         x_pool = ctx.enter_context(tc.tile_pool(name="x_pool", bufs=LOAD_BUFS))
         w_pool = ctx.enter_context(tc.tile_pool(name="w_pool", bufs=LOAD_BUFS))
         stage = ctx.enter_context(tc.tile_pool(name="stage", bufs=CHUNK))
-        codes = ctx.enter_context(tc.tile_pool(name="codes", bufs=3))
+        codes = ctx.enter_context(tc.tile_pool(name="codes", bufs=4))
         gates = ctx.enter_context(tc.tile_pool(name="gates", bufs=ROW_TILES))
         sums = ctx.enter_context(tc.psum_pool(name="sums", bufs=1))
         flips = ctx.enter_context(tc.psum_pool(name="flips", bufs=CHUNK))
@@ -133,7 +133,7 @@ def tile_lstmbaseline_pa_k_kernel(tc, x, W_ih0_words, W_ih0_scales, b_ih0, b_hh0
         sum_i = [sums.tile([P, H], F32, name="sum_i%d" % half) for half in range(ROW_TILES)]
 
         with tc.manual_schedule():
-            loaded_x = {0: load_x(0), 1: load_x(1)}
+            loaded_x = {0: load_x(0), 1: load_x(1), 2: load_x(2)}
 
             bias_rows = consts.tile([P, 4 * H], BF16)
             nc.vector.memset(bias_rows[:], 0.0)
@@ -162,13 +162,14 @@ def tile_lstmbaseline_pa_k_kernel(tc, x, W_ih0_words, W_ih0_scales, b_ih0, b_hh0
             bias_i = consts.tile([P, H], F32)
             nc.vector.tensor_copy(out=bias_i[:], in_=bias_i_psum[:])
 
-            coded_x = {0: transpose_and_quantise(loaded_x[0])}
+            coded_x = {0: transpose_and_quantise(loaded_x[0]), 1: transpose_and_quantise(loaded_x[1])}
             for c in range(CHUNKS):
-                if c + 2 < CHUNKS:
-                    loaded_x[c + 2] = load_x(c + 2)
+                if c + 3 < CHUNKS:
+                    loaded_x[c + 3] = load_x(c + 3)
                 if c + 1 < CHUNKS:
                     loaded_w[c + 1] = load_w(c + 1)
-                    coded_x[c + 1] = transpose_and_quantise(loaded_x[c + 1])
+                if c + 2 < CHUNKS:
+                    coded_x[c + 2] = transpose_and_quantise(loaded_x[c + 2])
                 multiply(c, coded_x[c][0], coded_x[c][1], loaded_w[c][0], loaded_w[c][1])
 
             a_go, gate_g, gate_o, a_i, gate_i, cell, tanh_cell, hidden = {}, {}, {}, {}, {}, {}, {}, {}

@@ -26,6 +26,10 @@ LOAD_GROUPS = 2
 
 LOAD_BUFS = 6
 
+TAIL_CHUNKS = 2
+BODY_CHUNKS = CHUNKS - TAIL_CHUNKS
+BODY_GROUPS = BODY_CHUNKS * CHUNK
+
 FLOPS = 2 * B * D * 3 * H
 BYTES = B * D * 2 + D * 3 * H + (D // 32) * 3 * H + 2 * 3 * H * 2 + B * H * 4
 
@@ -51,13 +55,40 @@ def tile_lstmbaseline_pa_k_kernel(tc, x, W_ih0_words, W_ih0_scales, b_ih0, b_hh0
             nc.sync.dma_start(out=x_rows[:], in_=x_view[:, :, c * CHUNK * K_PASS : (c + 1) * CHUNK * K_PASS])
             return x_rows
 
-        def load_w(c):
+        def load_w_planes(c):
             groups = slice(c * CHUNK, (c + 1) * CHUNK)
             for quadrant in range(4):
                 nc.gpsimd.dma_start(
                     out=w_planes[32 * quadrant : 32 * quadrant + CHUNK * PLANE_STEP, c, :].bitcast(F32),
                     in_=W_ih0_scales[groups, 4 * quadrant : 4 * quadrant + 4, :].bitcast(F32),
                 )
+
+        def load_w_tail():
+            tiles = {}
+            for c in range(BODY_CHUNKS, CHUNKS):
+                load_w_planes(c)
+                w_go = w_pool.tile([P, CHUNK, 2 * H], U32, align_bytes=64)
+                w_i = w_pool.tile([P, CHUNK, H], U32, align_bytes=64)
+                tiles[c] = (w_i, w_go)
+            for gate in range(3):
+                for c in range(BODY_CHUNKS, CHUNKS):
+                    for first in range(0, CHUNK, LOAD_GROUPS):
+                        here = slice(first, first + LOAD_GROUPS)
+                        there = slice(c * CHUNK + first, c * CHUNK + first + LOAD_GROUPS)
+                        if gate == 0:
+                            nc.sync.dma_start(
+                                out=tiles[c][0][:, here, :].bitcast(I32),
+                                in_=w_view[:, there, 0 : PACK * H].bitcast(I32),
+                            )
+                        else:
+                            nc.sync.dma_start(
+                                out=tiles[c][1][:, here, (gate - 1) * H : gate * H].bitcast(I32),
+                                in_=w_view[:, there, PACK * (gate + 1) * H : PACK * (gate + 2) * H].bitcast(I32),
+                            )
+            return tiles
+
+        def load_w(c):
+            load_w_planes(c)
             w_go = w_pool.tile([P, CHUNK, 2 * H], U32, align_bytes=64)
             for first in range(0, CHUNK, LOAD_GROUPS):
                 nc.sync.dma_start(
@@ -112,7 +143,7 @@ def tile_lstmbaseline_pa_k_kernel(tc, x, W_ih0_words, W_ih0_scales, b_ih0, b_hh0
                             rhs=w_go[:, j, :].bitcast(FP8X4),
                             rhs_scale=w_planes[j * PLANE_STEP : P, c, 2 * H : 4 * H],
                             start=(g == 0),
-                            stop=(g == GROUPS - 1),
+                            stop=(g == BODY_GROUPS - 1),
                         )
             for first in range(0, CHUNK, LOAD_GROUPS):
                 for half in range(ROW_TILES):
@@ -128,6 +159,29 @@ def tile_lstmbaseline_pa_k_kernel(tc, x, W_ih0_words, W_ih0_scales, b_ih0, b_hh0
                             start=(g == 0),
                             stop=(g == GROUPS - 1),
                         )
+
+        def multiply_tail(gate, sum_of_half):
+            for c in range(BODY_CHUNKS, CHUNKS):
+                x_words, x_planes = coded_x[c]
+                for first in range(0, CHUNK, LOAD_GROUPS):
+                    for half in range(ROW_TILES):
+                        rows = slice(half * P, (half + 1) * P)
+                        for j in range(first, first + LOAD_GROUPS):
+                            g = c * CHUNK + j
+                            if gate == 0:
+                                words = loaded_w[c][0][:, j, :]
+                            else:
+                                words = loaded_w[c][1][:, j, (gate - 1) * H : gate * H]
+                            column = 0 if gate == 0 else (gate + 1) * H
+                            nc.tensor.matmul_mx(
+                                out=sum_of_half[half][:],
+                                lhsT=x_words[:, j, rows].bitcast(FP8X4),
+                                lhsT_scale=x_planes[:, j, rows],
+                                rhs=words.bitcast(FP8X4),
+                                rhs_scale=w_planes[j * PLANE_STEP : P, c, column : column + H],
+                                start=(gate > 0 and g == BODY_GROUPS),
+                                stop=(g == GROUPS - 1),
+                            )
 
         sum_go = [sums.tile([P, 2 * H], F32, name="sum_go%d" % half) for half in range(ROW_TILES)]
         sum_i = [sums.tile([P, H], F32, name="sum_i%d" % half) for half in range(ROW_TILES)]
@@ -163,33 +217,50 @@ def tile_lstmbaseline_pa_k_kernel(tc, x, W_ih0_words, W_ih0_scales, b_ih0, b_hh0
             nc.vector.tensor_copy(out=bias_i[:], in_=bias_i_psum[:])
 
             coded_x = {0: transpose_and_quantise(loaded_x[0]), 1: transpose_and_quantise(loaded_x[1])}
-            for c in range(CHUNKS):
+            for c in range(BODY_CHUNKS):
                 if c + 3 < CHUNKS:
                     loaded_x[c + 3] = load_x(c + 3)
-                if c + 1 < CHUNKS:
+                if c + 1 < BODY_CHUNKS:
                     loaded_w[c + 1] = load_w(c + 1)
+                else:
+                    tail_tiles = load_w_tail()
+                    for late in range(BODY_CHUNKS, CHUNKS):
+                        loaded_w[late] = tail_tiles[late]
                 if c + 2 < CHUNKS:
                     coded_x[c + 2] = transpose_and_quantise(loaded_x[c + 2])
                 multiply(c, coded_x[c][0], coded_x[c][1], loaded_w[c][0], loaded_w[c][1])
 
-            a_go, gate_g, gate_o, a_i, gate_i, cell, tanh_cell, hidden = {}, {}, {}, {}, {}, {}, {}, {}
+            part_go = {}
             for half in range(ROW_TILES):
-                a_go[half] = gates.tile([P, 2 * H], F32, name="a_go")
-                nc.vector.tensor_add(out=a_go[half][:], in0=sum_go[half][:], in1=bias_go[:])
-                gate_g[half] = gates.tile([P, H], F32, name="gate_g")
-                nc.scalar.activation(out=gate_g[half][:], in_=a_go[half][:, 0:H], func=ACT.Tanh)
-                gate_o[half] = gates.tile([P, H], F32, name="gate_o")
-                nc.scalar.activation(out=gate_o[half][:], in_=a_go[half][:, H : 2 * H], func=ACT.Sigmoid)
+                part_go[half] = gates.tile([P, 2 * H], F32, name="part_go")
+                nc.vector.tensor_add(out=part_go[half][:], in0=sum_go[half][:], in1=bias_go[:])
+            multiply_tail(0, sum_i)
+            tail_g = [flips.tile([P, H], F32, tag="flipped", name="tail_g%d" % half) for half in range(ROW_TILES)]
+            multiply_tail(1, tail_g)
+            tail_o = [flips.tile([P, H], F32, tag="flipped", name="tail_o%d" % half) for half in range(ROW_TILES)]
+            multiply_tail(2, tail_o)
+
+            a_g, gate_g, a_o, gate_o, a_i, gate_i, cell, tanh_cell, hidden = {}, {}, {}, {}, {}, {}, {}, {}, {}
             for half in range(ROW_TILES):
                 a_i[half] = gates.tile([P, H], F32, name="a_i")
                 nc.vector.tensor_add(out=a_i[half][:], in0=sum_i[half][:], in1=bias_i[:])
                 gate_i[half] = gates.tile([P, H], F32, name="gate_i")
                 nc.scalar.activation(out=gate_i[half][:], in_=a_i[half][:], func=ACT.Sigmoid)
             for half in range(ROW_TILES):
+                a_g[half] = gates.tile([P, H], F32, name="a_g")
+                nc.vector.tensor_add(out=a_g[half][:], in0=tail_g[half][:], in1=part_go[half][:, 0:H])
+                gate_g[half] = gates.tile([P, H], F32, name="gate_g")
+                nc.scalar.activation(out=gate_g[half][:], in_=a_g[half][:], func=ACT.Tanh)
+            for half in range(ROW_TILES):
                 cell[half] = gates.tile([P, H], F32, name="cell")
                 nc.vector.tensor_mul(out=cell[half][:], in0=gate_i[half][:], in1=gate_g[half][:])
                 tanh_cell[half] = gates.tile([P, H], F32, name="tanh_cell")
                 nc.scalar.activation(out=tanh_cell[half][:], in_=cell[half][:], func=ACT.Tanh)
+            for half in range(ROW_TILES):
+                a_o[half] = gates.tile([P, H], F32, name="a_o")
+                nc.vector.tensor_add(out=a_o[half][:], in0=tail_o[half][:], in1=part_go[half][:, H : 2 * H])
+                gate_o[half] = gates.tile([P, H], F32, name="gate_o")
+                nc.scalar.activation(out=gate_o[half][:], in_=a_o[half][:], func=ACT.Sigmoid)
             for half in range(ROW_TILES):
                 hidden[half] = gates.tile([P, H], F32, name="hidden")
                 nc.vector.tensor_mul(out=hidden[half][:], in0=gate_o[half][:], in1=tanh_cell[half][:])

from contextlib import ExitStack

import concourse.mybir as mybir
from concourse.masks import make_identity

F32 = mybir.dt.float32
BF16 = mybir.dt.bfloat16
I32 = mybir.dt.int32
U32 = mybir.dt.uint32
U8 = mybir.dt.uint8
FP8X4 = mybir.dt.float8_e4m3fn_x4
ACT = mybir.ActivationFunctionType

P = 128
PACK = 4
K_PASS = P * PACK
PAIRS = K_PASS // 2

B, D, H = 256, 16384, 256
ROW_TILES = B // P
GROUPS = D // K_PASS
CHUNK = 4
CHUNKS = GROUPS // CHUNK
PLANE_STEP = 4
LOAD_GROUPS = 2

LOAD_BUFS = 6

TAIL_CHUNKS = 2
BODY_CHUNKS = CHUNKS - TAIL_CHUNKS
BODY_GROUPS = BODY_CHUNKS * CHUNK

FLOPS = 2 * B * D * 3 * H
BYTES = B * D * 2 + D * 3 * H + (D // 32) * 3 * H + 2 * 3 * H * 2 + B * H * 4


def tile_lstmbaseline_pa_k_kernel(tc, x, W_ih0_words, W_ih0_scales, b_ih0, b_hh0, out):
    nc = tc.nc

    x_view = x.rearrange("(b p) k -> p b k", p=P)
    w_view = W_ih0_words.rearrange("g p n t -> p g (n t)")

    with ExitStack() as ctx:
        consts = ctx.enter_context(tc.tile_pool(name="consts", bufs=1))
        x_pool = ctx.enter_context(tc.tile_pool(name="x_pool", bufs=LOAD_BUFS))
        w_pool = ctx.enter_context(tc.tile_pool(name="w_pool", bufs=LOAD_BUFS))
        stage = ctx.enter_context(tc.tile_pool(name="stage", bufs=CHUNK))
        codes = ctx.enter_context(tc.tile_pool(name="codes", bufs=4))
        gates = ctx.enter_context(tc.tile_pool(name="gates", bufs=ROW_TILES))
        sums = ctx.enter_context(tc.psum_pool(name="sums", bufs=1))
        flips = ctx.enter_context(tc.psum_pool(name="flips", bufs=CHUNK))

        def load_x(c):
            x_rows = x_pool.tile([P, ROW_TILES, CHUNK * K_PASS], BF16)
            nc.sync.dma_start(out=x_rows[:], in_=x_view[:, :, c * CHUNK * K_PASS : (c + 1) * CHUNK * K_PASS])
            return x_rows

        def load_w_planes(c):
            groups = slice(c * CHUNK, (c + 1) * CHUNK)
            for quadrant in range(4):
                nc.gpsimd.dma_start(
                    out=w_planes[32 * quadrant : 32 * quadrant + CHUNK * PLANE_STEP, c, :].bitcast(F32),
                    in_=W_ih0_scales[groups, 4 * quadrant : 4 * quadrant + 4, :].bitcast(F32),
                )

        def load_w_tail():
            tiles = {}
            for c in range(BODY_CHUNKS, CHUNKS):
                load_w_planes(c)
                w_go = w_pool.tile([P, CHUNK, 2 * H], U32, align_bytes=64)
                w_i = w_pool.tile([P, CHUNK, H], U32, align_bytes=64)
                tiles[c] = (w_i, w_go)
            for gate in range(3):
                for c in range(BODY_CHUNKS, CHUNKS):
                    for first in range(0, CHUNK, LOAD_GROUPS):
                        here = slice(first, first + LOAD_GROUPS)
                        there = slice(c * CHUNK + first, c * CHUNK + first + LOAD_GROUPS)
                        if gate == 0:
                            nc.sync.dma_start(
                                out=tiles[c][0][:, here, :].bitcast(I32),
                                in_=w_view[:, there, 0 : PACK * H].bitcast(I32),
                            )
                        else:
                            nc.sync.dma_start(
                                out=tiles[c][1][:, here, (gate - 1) * H : gate * H].bitcast(I32),
                                in_=w_view[:, there, PACK * (gate + 1) * H : PACK * (gate + 2) * H].bitcast(I32),
                            )
            return tiles

        def load_w(c):
            load_w_planes(c)
            w_go = w_pool.tile([P, CHUNK, 2 * H], U32, align_bytes=64)
            for first in range(0, CHUNK, LOAD_GROUPS):
                nc.sync.dma_start(
                    out=w_go[:, first : first + LOAD_GROUPS, :].bitcast(I32),
                    in_=w_view[
                        :, c * CHUNK + first : c * CHUNK + first + LOAD_GROUPS, PACK * 2 * H : PACK * 4 * H
                    ].bitcast(I32),
                )
            w_i = w_pool.tile([P, CHUNK, H], U32, align_bytes=64)
            for first in range(0, CHUNK, LOAD_GROUPS):
                nc.sync.dma_start(
                    out=w_i[:, first : first + LOAD_GROUPS, :].bitcast(I32),
                    in_=w_view[:, c * CHUNK + first : c * CHUNK + first + LOAD_GROUPS, 0 : PACK * H].bitcast(I32),
                )
            return w_i, w_go

        def transpose_and_quantise(x_rows):
            x_words = codes.tile([P, CHUNK, B], U32, align_bytes=64)
            x_planes = codes.tile([P, CHUNK, B], U8, align_bytes=64)
            banks = []
            for j in range(CHUNK):
                flipped = flips.tile([P, ROW_TILES, 2, P], F32)
                for half in range(ROW_TILES):
                    pairs = x_rows[:, half, :].bitcast(F32)
                    for odd in range(2):
                        nc.tensor.transpose(
                            flipped[:, half, odd, :],
                            pairs[:, j * PAIRS + odd : (j + 1) * PAIRS : 2],
                            identity[:],
                        )
                banks.append(flipped)
            for j in range(CHUNK):
                grouped = stage.tile([P, ROW_TILES, P, PACK], BF16, align_bytes=64)
                nc.scalar.copy(out=grouped[:].bitcast(F32), in_=banks[j][:].rearrange("p b u r -> p b r u"))
                nc.vector.quantize_mx(
                    out=x_words[:, j, :].bitcast(FP8X4),
                    scales=x_planes[:, j, :],
                    in_=grouped[:].rearrange("p b r t -> p (b r t)"),
                )
            return x_words, x_planes

        def multiply(c, x_words, x_planes, w_i, w_go):
            for first in range(0, CHUNK, LOAD_GROUPS):
                for half in range(ROW_TILES):
                    rows = slice(half * P, (half + 1) * P)
                    for j in range(first, first + LOAD_GROUPS):
                        g = c * CHUNK + j
                        nc.tensor.matmul_mx(
                            out=sum_go[half][:],
                            lhsT=x_words[:, j, rows].bitcast(FP8X4),
                            lhsT_scale=x_planes[:, j, rows],
                            rhs=w_go[:, j, :].bitcast(FP8X4),
                            rhs_scale=w_planes[j * PLANE_STEP : P, c, 2 * H : 4 * H],
                            start=(g == 0),
                            stop=(g == BODY_GROUPS - 1),
                        )
            for first in range(0, CHUNK, LOAD_GROUPS):
                for half in range(ROW_TILES):
                    rows = slice(half * P, (half + 1) * P)
                    for j in range(first, first + LOAD_GROUPS):
                        g = c * CHUNK + j
                        nc.tensor.matmul_mx(
                            out=sum_i[half][:],
                            lhsT=x_words[:, j, rows].bitcast(FP8X4),
                            lhsT_scale=x_planes[:, j, rows],
                            rhs=w_i[:, j, :].bitcast(FP8X4),
                            rhs_scale=w_planes[j * PLANE_STEP : P, c, 0:H],
                            start=(g == 0),
                            stop=(g == GROUPS - 1),
                        )

        def multiply_tail(gate, sum_of_half):
            for c in range(BODY_CHUNKS, CHUNKS):
                x_words, x_planes = coded_x[c]
                for first in range(0, CHUNK, LOAD_GROUPS):
                    for half in range(ROW_TILES):
                        rows = slice(half * P, (half + 1) * P)
                        for j in range(first, first + LOAD_GROUPS):
                            g = c * CHUNK + j
                            if gate == 0:
                                words = loaded_w[c][0][:, j, :]
                            else:
                                words = loaded_w[c][1][:, j, (gate - 1) * H : gate * H]
                            column = 0 if gate == 0 else (gate + 1) * H
                            nc.tensor.matmul_mx(
                                out=sum_of_half[half][:],
                                lhsT=x_words[:, j, rows].bitcast(FP8X4),
                                lhsT_scale=x_planes[:, j, rows],
                                rhs=words.bitcast(FP8X4),
                                rhs_scale=w_planes[j * PLANE_STEP : P, c, column : column + H],
                                start=(gate > 0 and g == BODY_GROUPS),
                                stop=(g == GROUPS - 1),
                            )

        sum_go = [sums.tile([P, 2 * H], F32, name="sum_go%d" % half) for half in range(ROW_TILES)]
        sum_i = [sums.tile([P, H], F32, name="sum_i%d" % half) for half in range(ROW_TILES)]

        with tc.manual_schedule():
            loaded_x = {0: load_x(0), 1: load_x(1), 2: load_x(2)}

            bias_rows = consts.tile([P, 4 * H], BF16)
            nc.vector.memset(bias_rows[:], 0.0)
            nc.scalar.dma_start(out=bias_rows[0:1, :], in_=b_ih0.unsqueeze(0))
            nc.scalar.dma_start(out=bias_rows[1:2, :], in_=b_hh0.unsqueeze(0))
            ones = consts.tile([P, P], BF16)
            nc.vector.memset(ones[:], 1.0)
            bias_go_psum = flips.tile([P, 2 * H], F32, tag="flipped")
            nc.tensor.matmul(out=bias_go_psum[:], lhsT=ones[:], rhs=bias_rows[:, 2 * H : 4 * H], start=True, stop=True)
            bias_i_psum = flips.tile([P, H], F32, tag="flipped")
            nc.tensor.matmul(out=bias_i_psum[:], lhsT=ones[:], rhs=bias_rows[:, 0:H], start=True, stop=True)

            w_planes = consts.tile([P, CHUNKS, 4 * H], U8, align_bytes=64)
            nc.vector.memset(w_planes[:].bitcast(I32), 0)
            identity = consts.tile([P, P], F32)
            make_identity(nc, identity[:])
            loaded_w = {0: load_w(0)}

            warm = consts.tile([P, 1], F32)
            nc.vector.memset(warm[:], 0.0)
            warmed = consts.tile([P, 1], F32)
            nc.scalar.activation(out=warmed[:], in_=warm[:], func=ACT.Sigmoid)

            bias_go = consts.tile([P, 2 * H], F32)
            nc.vector.tensor_copy(out=bias_go[:], in_=bias_go_psum[:])
            bias_i = consts.tile([P, H], F32)
            nc.vector.tensor_copy(out=bias_i[:], in_=bias_i_psum[:])

            coded_x = {0: transpose_and_quantise(loaded_x[0]), 1: transpose_and_quantise(loaded_x[1])}
            for c in range(BODY_CHUNKS):
                if c + 3 < CHUNKS:
                    loaded_x[c + 3] = load_x(c + 3)
                if c + 1 < BODY_CHUNKS:
                    loaded_w[c + 1] = load_w(c + 1)
                else:
                    tail_tiles = load_w_tail()
                    for late in range(BODY_CHUNKS, CHUNKS):
                        loaded_w[late] = tail_tiles[late]
                if c + 2 < CHUNKS:
                    coded_x[c + 2] = transpose_and_quantise(loaded_x[c + 2])
                multiply(c, coded_x[c][0], coded_x[c][1], loaded_w[c][0], loaded_w[c][1])

            part_go = {}
            for half in range(ROW_TILES):
                part_go[half] = gates.tile([P, 2 * H], F32, name="part_go")
                nc.vector.tensor_add(out=part_go[half][:], in0=sum_go[half][:], in1=bias_go[:])
            multiply_tail(0, sum_i)
            tail_g = [flips.tile([P, H], F32, tag="flipped", name="tail_g%d" % half) for half in range(ROW_TILES)]
            multiply_tail(1, tail_g)
            tail_o = [flips.tile([P, H], F32, tag="flipped", name="tail_o%d" % half) for half in range(ROW_TILES)]
            multiply_tail(2, tail_o)

            a_g, gate_g, a_o, gate_o, a_i, gate_i, cell, tanh_cell, hidden = {}, {}, {}, {}, {}, {}, {}, {}, {}
            for half in range(ROW_TILES):
                a_i[half] = gates.tile([P, H], F32, name="a_i")
                nc.vector.tensor_add(out=a_i[half][:], in0=sum_i[half][:], in1=bias_i[:])
                gate_i[half] = gates.tile([P, H], F32, name="gate_i")
                nc.scalar.activation(out=gate_i[half][:], in_=a_i[half][:], func=ACT.Sigmoid)
            for half in range(ROW_TILES):
                a_g[half] = gates.tile([P, H], F32, name="a_g")
                nc.vector.tensor_add(out=a_g[half][:], in0=tail_g[half][:], in1=part_go[half][:, 0:H])
                gate_g[half] = gates.tile([P, H], F32, name="gate_g")
                nc.scalar.activation(out=gate_g[half][:], in_=a_g[half][:], func=ACT.Tanh)
            for half in range(ROW_TILES):
                cell[half] = gates.tile([P, H], F32, name="cell")
                nc.vector.tensor_mul(out=cell[half][:], in0=gate_i[half][:], in1=gate_g[half][:])
                tanh_cell[half] = gates.tile([P, H], F32, name="tanh_cell")
                nc.scalar.activation(out=tanh_cell[half][:], in_=cell[half][:], func=ACT.Tanh)
            for half in range(ROW_TILES):
                a_o[half] = gates.tile([P, H], F32, name="a_o")
                nc.vector.tensor_add(out=a_o[half][:], in0=tail_o[half][:], in1=part_go[half][:, H : 2 * H])
                gate_o[half] = gates.tile([P, H], F32, name="gate_o")
                nc.scalar.activation(out=gate_o[half][:], in_=a_o[half][:], func=ACT.Sigmoid)
            for half in range(ROW_TILES):
                hidden[half] = gates.tile([P, H], F32, name="hidden")
                nc.vector.tensor_mul(out=hidden[half][:], in0=gate_o[half][:], in1=tanh_cell[half][:])
                nc.sync.dma_start(out=out[half * P : (half + 1) * P, :], in_=hidden[half][:])
